import numpy as np
import ml_dtypes


def mxq(x, axis, fmt="e4m3"):
    dtype, down = {"e4m3": (ml_dtypes.float8_e4m3fn, 7), "e5m2": (ml_dtypes.float8_e5m2, 14)}[fmt]
    v = np.moveaxis(np.asarray(x, np.float32).astype(ml_dtypes.bfloat16).astype(np.float64), axis, -1)
    blocks = v.reshape(v.shape[:-1] + (-1, 32))
    amax = np.abs(blocks).max(-1, keepdims=True)
    byte = np.maximum(np.where(amax > 0, np.frexp(amax)[1] - 1 + 127, 0) - down, 1)
    scale = np.exp2(byte - 127.0)
    codes = (blocks / scale).astype(np.float32).astype(dtype).astype(np.float64)
    return np.moveaxis((codes * scale).reshape(v.shape), -1, axis)


WIDE = False


def mx_kscale(k):
    if not WIDE:
        return np.ones(k)
    levels = np.array([10, -10, 5, -5, 0])
    a = np.random.permutation(np.resize(levels, k // 512 * 4)).reshape(k // 512, 4)
    idx = np.arange(k)
    return np.exp2(a[idx // 512, idx % 128 // 32])


BF16 = ml_dtypes.bfloat16


def bf(x):
    return np.asarray(x, np.float32).astype(BF16)


def f64(x):
    return np.asarray(x).astype(np.float64)


B, NW, N, D, J = 4, 4, 512, 128, 3
KEEP = (0.0625, 0.0625, 0.25, 1.0)


def draw_power(j, a):
    r = np.random.uniform(size=(B, NW, N, N)) * (np.random.uniform(size=(B, NW, N, N)) < KEEP[j])
    t = r / r.sum(-1, keepdims=True)
    c = 0.5 ** (2 ** j)
    p = c * np.eye(N) + (1.0 - c) * t
    return bf(p * a[:, None] / a[None, :])


def setup_inputs():
    s = mx_kscale(N)
    a = s / s.max()
    alpha = np.random.uniform(size=(NW, D))
    x = np.random.standard_normal((B, NW, N, D)) * alpha[None, :, None, :] * a[:, None]
    return {"x_nodes": bf(x), "p1": draw_power(0, a), "p2": draw_power(1, a), "p4": draw_power(2, a), "p8": draw_power(3, a)}


def reference(x_nodes, p1, p2, p4, p8):
    X = f64(x_nodes)
    powers = [f64(p1), f64(p2), f64(p4), f64(p8)]
    psi = [mxq(powers[j] - powers[j + 1], 3, "e4m3") for j in range(J)]
    Xq = mxq(X, 2, "e4m3")
    first = [np.abs(psi[j] @ Xq) for j in range(J)]
    firstq = [mxq(first[j], 2, "e4m3") for j in range(J - 1)]
    second = [np.abs(psi[k] @ firstq[j]) for j in range(J) for k in range(j + 1, J)]
    feats = np.concatenate([X] + first + second, axis=-1)
    pooled = feats.mean(axis=2)
    return pooled.reshape(B, -1)

@@ -1,0 +1,225 @@
+from contextlib import ExitStack
+
+import concourse.mybir as mybir
+from concourse.masks import make_identity
+
+F32 = mybir.dt.float32
+BF16 = mybir.dt.bfloat16
+U32 = mybir.dt.uint32
+U8 = mybir.dt.uint8
+FP8X4 = mybir.dt.float8_e4m3fn_x4
+ABS = mybir.ActivationFunctionType.Abs
+COPY = mybir.ActivationFunctionType.Copy
+
+CLOUDS = 4
+WEIGHTINGS = 4
+SETS = CLOUDS * WEIGHTINGS
+POINTS = 512
+FEATS = 128
+P = 128
+SLOTS = 4
+HALVES = 2
+WAVELETS = 3
+BLOCKS = 7
+BANK = 512
+ROW_TILES_PER_BANK = BANK // (HALVES * P)
+ONES_COLS = 32
+LOADS_AHEAD = 3
+
+FLOPS = 2 * POINTS * POINTS * FEATS * 6 * SETS
+
+
+def tile_simplicialfeatlearninglayertri_pb_t_kernel(tc, x_nodes, p1, p2, p4, p8, out):
+    nc = tc.nc
+    operators = (p1, p2, p4, p8)
+
+    with ExitStack() as ctx:
+        const = ctx.enter_context(tc.tile_pool(name="const", bufs=1))
+        load = ctx.enter_context(tc.tile_pool(name="load", bufs=LOADS_AHEAD))
+        work = ctx.enter_context(tc.tile_pool(name="work", bufs=2))
+        pair_psum = ctx.enter_context(tc.psum_pool(name="pair_psum", bufs=4))
+        mx_psum = ctx.enter_context(tc.psum_pool(name="mx_psum", bufs=4))
+
+        identity = const.tile([P, P], F32)
+        make_identity(nc, identity[:])
+        ones = const.tile([P, ONES_COLS], BF16)
+        nc.vector.memset(ones[:], 1.0)
+        sums = const.tile([P, P], F32)
+        nc.vector.memset(sums[:], 0.0)
+        sums_by_set = sums[:, 0 : SETS * BLOCKS].rearrange("d (s i) -> d s i", i=BLOCKS)
+
+        x_rows, x_mx = {}, {}
+        power_rows, psi_rows, psi_grouped, psi_mx, f_grouped, f_mx = {}, {}, {}, {}, {}, {}
+
+        def load_cloud(b):
+            rows = work.tile([P, WEIGHTINGS * SLOTS * FEATS], BF16, tag="x_rows")
+            nc.sync.dma_start(
+                out=rows[:].rearrange("c (g r) -> c g r", r=2 * FEATS),
+                in_=x_nodes[b].rearrange("w (u c e) d -> c (w u) (e d)", u=HALVES, e=2),
+            )
+            x_rows[b] = rows
+
+        def prepare_cloud(b):
+            rows = x_rows[b]
+            grouped = work.tile([P, WEIGHTINGS * FEATS * SLOTS], BF16, tag="x_grouped", align_bytes=64)
+            nc.vector.tensor_copy(
+                out=grouped[:].rearrange("c (w d t) -> c w d t", w=WEIGHTINGS, t=SLOTS),
+                in_=rows[:].rearrange("c (w t d) -> c w d t", w=WEIGHTINGS, t=SLOTS),
+            )
+            codes = work.tile([P, WEIGHTINGS * FEATS], U32, tag="x_codes", align_bytes=64)
+            scales = work.tile([P, WEIGHTINGS * FEATS], U8, tag="x_scales", align_bytes=64)
+            nc.vector.quantize_mx(out=codes[:].bitcast(FP8X4), scales=scales[:], in_=grouped[:])
+            x_mx[b] = (codes, scales)
+
+            bank = mx_psum.tile([P, BANK], F32, tag="mx")
+            for w in range(WEIGHTINGS):
+                for t in range(SLOTS):
+                    first = (w * SLOTS + t) * FEATS
+                    nc.tensor.matmul(
+                        out=bank[:, w * ONES_COLS : (w + 1) * ONES_COLS],
+                        lhsT=rows[:, first : first + FEATS],
+                        rhs=ones[:],
+                        start=(t == 0),
+                        stop=(t == SLOTS - 1),
+                    )
+            nc.scalar.copy(
+                out=sums_by_set[:, b * WEIGHTINGS : (b + 1) * WEIGHTINGS, 0],
+                in_=bank[:, 0 : WEIGHTINGS * ONES_COLS].rearrange("d (w r) -> d w r", r=ONES_COLS)[:, :, 0],
+            )
+
+        def load_set(s):
+            b, w = divmod(s, WEIGHTINGS)
+            power_rows[s] = []
+            for j, operator in enumerate(operators):
+                rows = load.tile([P, SLOTS * POINTS], BF16, tag="power%d" % j)
+                nc.sync.dma_start(
+                    out=rows[:].rearrange("q (u r) -> q u r", u=HALVES),
+                    in_=operator[b, w].rearrange("(u q e) m -> q u (e m)", u=HALVES, e=2),
+                )
+                power_rows[s].append(rows)
+
+        def subtract(s):
+            psi_rows[s] = []
+            for j in range(WAVELETS):
+                rows = work.tile([P, SLOTS * POINTS], BF16, tag="psi%d" % j)
+                nc.vector.tensor_sub(out=rows[:], in0=power_rows[s][j][:], in1=power_rows[s][j + 1][:])
+                psi_rows[s].append(rows)
+
+        def transpose(s):
+            psi_grouped[s] = []
+            for j in range(WAVELETS):
+                pairs = psi_rows[s][j][:].bitcast(F32)
+                grouped = work.tile([P, POINTS * SLOTS], BF16, tag="grouped%d" % j, align_bytes=64)
+                grouped_pairs = grouped[:].bitcast(F32)
+                for h in range(SLOTS // ROW_TILES_PER_BANK):
+                    bank = pair_psum.tile([P, BANK], F32, tag="pairs")
+                    for i in range(BANK // P):
+                        first = h * BANK + i * P
+                        nc.tensor.transpose(
+                            out=bank[:, i * P : (i + 1) * P],
+                            in_=pairs[:, first : first + P],
+                            identity=identity[:],
+                        )
+                    copy = nc.vector.tensor_copy if (j * 2 + h) % 3 == 1 else nc.scalar.copy
+                    copy(
+                        out=grouped_pairs[:, h * BANK : (h + 1) * BANK].rearrange(
+                            "c (a q u) -> c a q u", a=ROW_TILES_PER_BANK, u=HALVES
+                        ),
+                        in_=bank[:].rearrange("c (a u q) -> c a q u", a=ROW_TILES_PER_BANK, u=HALVES),
+                    )
+                psi_grouped[s].append(grouped)
+
+        def quantise_psi(s):
+            psi_mx[s] = []
+            for j in range(WAVELETS):
+                codes = work.tile([P, POINTS], U32, tag="psi_codes%d" % j, align_bytes=64)
+                scales = work.tile([P, POINTS], U8, tag="psi_scales%d" % j, align_bytes=64)
+                nc.vector.quantize_mx(
+                    out=codes[:].bitcast(FP8X4), scales=scales[:], in_=psi_grouped[s][j][:]
+                )
+                psi_mx[s].append((codes, scales))
+
+        def mx_pass(acc, stationary, stationary_cols, moving, moving_cols):
+            nc.tensor.matmul_mx(
+                out=acc,
+                lhsT=stationary[0][:, stationary_cols].bitcast(FP8X4),
+                lhsT_scale=stationary[1][:, stationary_cols],
+                rhs=moving[0][:, moving_cols].bitcast(FP8X4),
+                rhs_scale=moving[1][:, moving_cols],
+                start=True,
+                stop=True,
+            )
+
+        def pool_product(s, block, features, feature_cols, psi):
+            bank = mx_psum.tile([P, BANK], F32, tag="mx")
+            mx_pass(bank[:], features, feature_cols, psi, slice(0, POINTS))
+            absolute = work.tile([P, BANK], BF16, tag="absolute")
+            nc.scalar.activation(
+                out=absolute[:], in_=bank[:], func=ABS, accum_out=sums_by_set[:, s, block : block + 1]
+            )
+
+        def first_layer(s):
+            b, w = divmod(s, WEIGHTINGS)
+            x_cols = slice(w * FEATS, (w + 1) * FEATS)
+            grouped = work.tile([P, 2 * FEATS * SLOTS], BF16, tag="f_grouped", align_bytes=64)
+            for j in range(2):
+                bank = mx_psum.tile([P, BANK], F32, tag="mx")
+                for t in range(SLOTS):
+                    cols = slice(t * P, (t + 1) * P)
+                    mx_pass(bank[:, cols], psi_mx[s][j], cols, x_mx[b], x_cols)
+                nc.scalar.activation(
+                    out=grouped[:, j * BANK : (j + 1) * BANK].rearrange("c (d t) -> c d t", t=SLOTS),
+                    in_=bank[:].rearrange("c (t d) -> c d t", t=SLOTS),
+                    func=ABS,
+                )
+            f_grouped[s] = grouped
+            for j in range(WAVELETS):
+                pool_product(s, 1 + j, x_mx[b], x_cols, psi_mx[s][j])
+
+        def quantise_f(s):
+            codes = work.tile([P, 2 * FEATS], U32, tag="f_codes", align_bytes=64)
+            scales = work.tile([P, 2 * FEATS], U8, tag="f_scales", align_bytes=64)
+            nc.vector.quantize_mx(out=codes[:].bitcast(FP8X4), scales=scales[:], in_=f_grouped[s][:])
+            f_mx[s] = (codes, scales)
+
+        def second_layer(s):
+            block = 1 + WAVELETS
+            for j in range(WAVELETS):
+                for k in range(j + 1, WAVELETS):
+                    pool_product(s, block, f_mx[s], slice(j * FEATS, (j + 1) * FEATS), psi_mx[s][k])
+                    block += 1
+
+        def load_ahead(s):
+            if s < SETS:
+                if s % WEIGHTINGS == 0:
+                    load_cloud(s // WEIGHTINGS)
+                load_set(s)
+
+        for s in range(LOADS_AHEAD):
+            load_ahead(s)
+        prepare_cloud(0)
+        subtract(0)
+        transpose(0)
+        quantise_psi(0)
+        for s in range(SETS):
+            following = s + 1
+            load_ahead(s + LOADS_AHEAD)
+            if following < SETS:
+                subtract(following)
+            first_layer(s)
+            if following < SETS:
+                transpose(following)
+            quantise_f(s)
+            if following < SETS:
+                quantise_psi(following)
+            if s % WEIGHTINGS == WEIGHTINGS - 2 and s + 2 < SETS:
+                prepare_cloud((s + 2) // WEIGHTINGS)
+            second_layer(s)
+
+        bank = mx_psum.tile([P, BANK], F32, tag="mx")
+        nc.tensor.transpose(out=bank[:, 0:P], in_=sums[:], identity=identity[:])
+        means = const.tile([P, FEATS], F32)
+        nc.scalar.activation(out=means[:], in_=bank[:, 0:P], func=COPY, scale=1.0 / POINTS)
+        nc.sync.dma_start(
+            out=out.rearrange("b (r d) -> (b r) d", d=FEATS), in_=means[0 : SETS * BLOCKS, :]
+        )

@@ -39,6 +39,7 @@ def tile_simplicialfeatlearninglayertri_pb_t_kernel(tc, x_nodes, p1, p2, p4, p8,
         work = ctx.enter_context(tc.tile_pool(name="work", bufs=2))
         pair_psum = ctx.enter_context(tc.psum_pool(name="pair_psum", bufs=4))
         mx_psum = ctx.enter_context(tc.psum_pool(name="mx_psum", bufs=4))
+        ctx.enter_context(tc.manual_schedule())
 
         identity = const.tile([P, P], F32)
         make_identity(nc, identity[:])

@@ -19,12 +19,14 @@ FEATS = 128
 P = 128
 SLOTS = 4
 HALVES = 2
+ROWS = POINTS // P
 WAVELETS = 3
 BLOCKS = 7
 BANK = 512
-ROW_TILES_PER_BANK = BANK // (HALVES * P)
+QUARTERS = BANK // P
 ONES_COLS = 32
 LOADS_AHEAD = 3
+OPERATOR_ORDER = (1, 0, 2, 3)
 
 FLOPS = 2 * POINTS * POINTS * FEATS * 6 * SETS
 
@@ -37,9 +39,8 @@ def tile_simplicialfeatlearninglayertri_pb_t_kernel(tc, x_nodes, p1, p2, p4, p8,
         const = ctx.enter_context(tc.tile_pool(name="const", bufs=1))
         load = ctx.enter_context(tc.tile_pool(name="load", bufs=LOADS_AHEAD))
         work = ctx.enter_context(tc.tile_pool(name="work", bufs=2))
-        pair_psum = ctx.enter_context(tc.psum_pool(name="pair_psum", bufs=4))
-        mx_psum = ctx.enter_context(tc.psum_pool(name="mx_psum", bufs=4))
-        ctx.enter_context(tc.manual_schedule())
+        pair_psum = ctx.enter_context(tc.psum_pool(name="pair_psum", bufs=5))
+        mx_psum = ctx.enter_context(tc.psum_pool(name="mx_psum", bufs=3))
 
         identity = const.tile([P, P], F32)
         make_identity(nc, identity[:])
@@ -50,7 +51,7 @@ def tile_simplicialfeatlearninglayertri_pb_t_kernel(tc, x_nodes, p1, p2, p4, p8,
         sums_by_set = sums[:, 0 : SETS * BLOCKS].rearrange("d (s i) -> d s i", i=BLOCKS)
 
         x_rows, x_mx = {}, {}
-        power_rows, psi_rows, psi_grouped, psi_mx, f_grouped, f_mx = {}, {}, {}, {}, {}, {}
+        power_rows, psi_grouped, psi_mx, f_rows, f_mx = {}, {}, {}, {}, {}
 
         def load_cloud(b):
             rows = work.tile([P, WEIGHTINGS * SLOTS * FEATS], BF16, tag="x_rows")
@@ -90,45 +91,58 @@ def tile_simplicialfeatlearninglayertri_pb_t_kernel(tc, x_nodes, p1, p2, p4, p8,
 
         def load_set(s):
             b, w = divmod(s, WEIGHTINGS)
-            power_rows[s] = []
-            for j, operator in enumerate(operators):
-                rows = load.tile([P, SLOTS * POINTS], BF16, tag="power%d" % j)
+            power_rows[s] = {}
+            for j in OPERATOR_ORDER:
+                rows = load.tile([P, ROWS * POINTS], BF16, tag="power%d" % j)
                 nc.sync.dma_start(
-                    out=rows[:].rearrange("q (u r) -> q u r", u=HALVES),
-                    in_=operator[b, w].rearrange("(u q e) m -> q u (e m)", u=HALVES, e=2),
+                    out=rows[:].rearrange("q (v r) -> q v r", v=HALVES),
+                    in_=operators[j][b, w].rearrange("(v q i) m -> q v (i m)", v=HALVES, i=2),
                 )
-                power_rows[s].append(rows)
+                power_rows[s][j] = rows
 
-        def subtract(s):
-            psi_rows[s] = []
-            for j in range(WAVELETS):
-                rows = work.tile([P, SLOTS * POINTS], BF16, tag="psi%d" % j)
-                nc.vector.tensor_sub(out=rows[:], in0=power_rows[s][j][:], in1=power_rows[s][j + 1][:])
-                psi_rows[s].append(rows)
+        def transpose_pairs(pairs):
+            bank = pair_psum.tile([P, BANK], F32, tag="pairs")
+            for g in range(QUARTERS):
+                cols = slice(g * P, (g + 1) * P)
+                nc.tensor.transpose(out=bank[:, cols], in_=pairs[:, cols], identity=identity[:])
+            return bank
 
-        def transpose(s):
-            psi_grouped[s] = []
-            for j in range(WAVELETS):
-                pairs = psi_rows[s][j][:].bitcast(F32)
-                grouped = work.tile([P, POINTS * SLOTS], BF16, tag="grouped%d" % j, align_bytes=64)
-                grouped_pairs = grouped[:].bitcast(F32)
-                for h in range(SLOTS // ROW_TILES_PER_BANK):
-                    bank = pair_psum.tile([P, BANK], F32, tag="pairs")
-                    for i in range(BANK // P):
-                        first = h * BANK + i * P
-                        nc.tensor.transpose(
-                            out=bank[:, i * P : (i + 1) * P],
-                            in_=pairs[:, first : first + P],
-                            identity=identity[:],
-                        )
-                    copy = nc.vector.tensor_copy if (j * 2 + h) % 3 == 1 else nc.scalar.copy
-                    copy(
-                        out=grouped_pairs[:, h * BANK : (h + 1) * BANK].rearrange(
-                            "c (a q u) -> c a q u", a=ROW_TILES_PER_BANK, u=HALVES
-                        ),
-                        in_=bank[:].rearrange("c (a u q) -> c a q u", a=ROW_TILES_PER_BANK, u=HALVES),
-                    )
-                psi_grouped[s].append(grouped)
+        def half_cols(v):
+            return slice(v * 2 * BANK, (v + 1) * 2 * BANK)
+
+        def transpose_operator(s, j):
+            pairs = power_rows[s][j][:].bitcast(F32)
+            return [transpose_pairs(pairs[:, v * BANK : (v + 1) * BANK]) for v in range(HALVES)]
+
+        def move_to_sbuf(banks, tag):
+            moved = work.tile([P, POINTS * SLOTS], BF16, tag=tag)
+            for v in range(HALVES):
+                nc.scalar.copy(
+                    out=moved[:, half_cols(v)].bitcast(F32).rearrange("c (q g) -> c q g", g=QUARTERS),
+                    in_=banks[v][:].rearrange("c (g q) -> c q g", g=QUARTERS),
+                )
+            return moved
+
+        def in_sbuf(values, v):
+            return values[:, half_cols(v)].rearrange("c (q g e) -> c q g e", g=QUARTERS, e=2)
+
+        def in_psum(banks, v):
+            return banks[v][:].bitcast(BF16).rearrange("c (g q e) -> c q g e", g=QUARTERS, e=2)
+
+        def make_wavelets(s):
+            psi0 = work.tile([P, POINTS * SLOTS], BF16, tag="psi0", align_bytes=64)
+            psi1 = work.tile([P, POINTS * SLOTS], BF16, tag="psi1", align_bytes=64)
+            psi2 = work.tile([P, POINTS * SLOTS], BF16, tag="psi2", align_bytes=64)
+            p2_sbuf = move_to_sbuf(transpose_operator(s, 1), "p2_sbuf")
+            p1_psum = transpose_operator(s, 0)
+            for v in range(HALVES):
+                nc.vector.tensor_sub(out=in_sbuf(psi0, v), in0=in_psum(p1_psum, v), in1=in_sbuf(p2_sbuf, v))
+            p4_sbuf = move_to_sbuf(transpose_operator(s, 2), "p4_sbuf")
+            nc.vector.tensor_sub(out=psi1[:], in0=p2_sbuf[:], in1=p4_sbuf[:])
+            p8_psum = transpose_operator(s, 3)
+            for v in range(HALVES):
+                nc.vector.tensor_sub(out=in_sbuf(psi2, v), in0=in_sbuf(p4_sbuf, v), in1=in_psum(p8_psum, v))
+            psi_grouped[s] = (psi0, psi1, psi2)
 
         def quantise_psi(s):
             psi_mx[s] = []
@@ -140,54 +154,51 @@ def tile_simplicialfeatlearninglayertri_pb_t_kernel(tc, x_nodes, p1, p2, p4, p8,
                 )
                 psi_mx[s].append((codes, scales))
 
-        def mx_pass(acc, stationary, stationary_cols, moving, moving_cols):
+        def pool_product(s, block, features, feature_cols, psi, absolute):
+            bank = mx_psum.tile([P, BANK], F32, tag="mx")
             nc.tensor.matmul_mx(
-                out=acc,
-                lhsT=stationary[0][:, stationary_cols].bitcast(FP8X4),
-                lhsT_scale=stationary[1][:, stationary_cols],
-                rhs=moving[0][:, moving_cols].bitcast(FP8X4),
-                rhs_scale=moving[1][:, moving_cols],
+                out=bank[:],
+                lhsT=features[0][:, feature_cols].bitcast(FP8X4),
+                lhsT_scale=features[1][:, feature_cols],
+                rhs=psi[0][:].bitcast(FP8X4),
+                rhs_scale=psi[1][:],
                 start=True,
                 stop=True,
             )
-
-        def pool_product(s, block, features, feature_cols, psi):
-            bank = mx_psum.tile([P, BANK], F32, tag="mx")
-            mx_pass(bank[:], features, feature_cols, psi, slice(0, POINTS))
-            absolute = work.tile([P, BANK], BF16, tag="absolute")
             nc.scalar.activation(
-                out=absolute[:], in_=bank[:], func=ABS, accum_out=sums_by_set[:, s, block : block + 1]
+                out=absolute, in_=bank[:], func=ABS, accum_out=sums_by_set[:, s, block : block + 1]
             )
+
+        def unread():
+            absolute = work.tile([P, POINTS], BF16, tag="unread")
+            return absolute[:]
 
         def first_layer(s):
             b, w = divmod(s, WEIGHTINGS)
             x_cols = slice(w * FEATS, (w + 1) * FEATS)
-            grouped = work.tile([P, 2 * FEATS * SLOTS], BF16, tag="f_grouped", align_bytes=64)
-            for j in range(2):
-                bank = mx_psum.tile([P, BANK], F32, tag="mx")
-                for t in range(SLOTS):
-                    cols = slice(t * P, (t + 1) * P)
-                    mx_pass(bank[:, cols], psi_mx[s][j], cols, x_mx[b], x_cols)
-                nc.scalar.activation(
-                    out=grouped[:, j * BANK : (j + 1) * BANK].rearrange("c (d t) -> c d t", t=SLOTS),
-                    in_=bank[:].rearrange("c (t d) -> c d t", t=SLOTS),
-                    func=ABS,
-                )
-            f_grouped[s] = grouped
-            for j in range(WAVELETS):
-                pool_product(s, 1 + j, x_mx[b], x_cols, psi_mx[s][j])
+            rows = work.tile([P, 2 * POINTS], BF16, tag="f_rows")
+            pool_product(s, 1, x_mx[b], x_cols, psi_mx[s][0], rows[:, 0:POINTS])
+            pool_product(s, 2, x_mx[b], x_cols, psi_mx[s][1], rows[:, POINTS : 2 * POINTS])
+            pool_product(s, 3, x_mx[b], x_cols, psi_mx[s][2], unread())
+            f_rows[s] = rows
 
         def quantise_f(s):
+            bank = transpose_pairs(f_rows[s][:].bitcast(F32))
+            grouped = work.tile([P, 2 * FEATS * SLOTS], BF16, tag="f_grouped", align_bytes=64)
+            nc.scalar.copy(
+                out=grouped[:].bitcast(F32).rearrange("c (j d u) -> c j d u", j=2, u=HALVES),
+                in_=bank[:].rearrange("c (j u d) -> c j d u", j=2, u=HALVES),
+            )
             codes = work.tile([P, 2 * FEATS], U32, tag="f_codes", align_bytes=64)
             scales = work.tile([P, 2 * FEATS], U8, tag="f_scales", align_bytes=64)
-            nc.vector.quantize_mx(out=codes[:].bitcast(FP8X4), scales=scales[:], in_=f_grouped[s][:])
+            nc.vector.quantize_mx(out=codes[:].bitcast(FP8X4), scales=scales[:], in_=grouped[:])
             f_mx[s] = (codes, scales)
 
         def second_layer(s):
             block = 1 + WAVELETS
             for j in range(WAVELETS):
                 for k in range(j + 1, WAVELETS):
-                    pool_product(s, block, f_mx[s], slice(j * FEATS, (j + 1) * FEATS), psi_mx[s][k])
+                    pool_product(s, block, f_mx[s], slice(j * FEATS, (j + 1) * FEATS), psi_mx[s][k], unread())
                     block += 1
 
         def load_ahead(s):
@@ -199,17 +210,14 @@ def tile_simplicialfeatlearninglayertri_pb_t_kernel(tc, x_nodes, p1, p2, p4, p8,
         for s in range(LOADS_AHEAD):
             load_ahead(s)
         prepare_cloud(0)
-        subtract(0)
-        transpose(0)
+        make_wavelets(0)
         quantise_psi(0)
         for s in range(SETS):
             following = s + 1
             load_ahead(s + LOADS_AHEAD)
             if following < SETS:
-                subtract(following)
+                make_wavelets(following)
             first_layer(s)
-            if following < SETS:
-                transpose(following)
             quantise_f(s)
             if following < SETS:
                 quantise_psi(following)

from contextlib import ExitStack

import concourse.mybir as mybir
from concourse.masks import make_identity

F32 = mybir.dt.float32
BF16 = mybir.dt.bfloat16
U32 = mybir.dt.uint32
U8 = mybir.dt.uint8
FP8X4 = mybir.dt.float8_e4m3fn_x4
ABS = mybir.ActivationFunctionType.Abs
COPY = mybir.ActivationFunctionType.Copy

CLOUDS = 4
WEIGHTINGS = 4
SETS = CLOUDS * WEIGHTINGS
POINTS = 512
FEATS = 128
P = 128
SLOTS = 4
HALVES = 2
ROWS = POINTS // P
WAVELETS = 3
BLOCKS = 7
BANK = 512
QUARTERS = BANK // P
ONES_COLS = 32
LOADS_AHEAD = 3
OPERATOR_ORDER = (1, 0, 2, 3)

FLOPS = 2 * POINTS * POINTS * FEATS * 6 * SETS


def tile_simplicialfeatlearninglayertri_pb_t_kernel(tc, x_nodes, p1, p2, p4, p8, out):
    nc = tc.nc
    operators = (p1, p2, p4, p8)

    with ExitStack() as ctx:
        const = ctx.enter_context(tc.tile_pool(name="const", bufs=1))
        load = ctx.enter_context(tc.tile_pool(name="load", bufs=LOADS_AHEAD))
        work = ctx.enter_context(tc.tile_pool(name="work", bufs=2))
        pair_psum = ctx.enter_context(tc.psum_pool(name="pair_psum", bufs=5))
        mx_psum = ctx.enter_context(tc.psum_pool(name="mx_psum", bufs=3))

        identity = const.tile([P, P], F32)
        make_identity(nc, identity[:])
        ones = const.tile([P, ONES_COLS], BF16)
        nc.vector.memset(ones[:], 1.0)
        sums = const.tile([P, P], F32)
        nc.vector.memset(sums[:], 0.0)
        sums_by_set = sums[:, 0 : SETS * BLOCKS].rearrange("d (s i) -> d s i", i=BLOCKS)

        x_rows, x_mx = {}, {}
        power_rows, psi_grouped, psi_mx, f_rows, f_mx = {}, {}, {}, {}, {}

        def load_cloud(b):
            rows = work.tile([P, WEIGHTINGS * SLOTS * FEATS], BF16, tag="x_rows")
            nc.sync.dma_start(
                out=rows[:].rearrange("c (g r) -> c g r", r=2 * FEATS),
                in_=x_nodes[b].rearrange("w (u c e) d -> c (w u) (e d)", u=HALVES, e=2),
            )
            x_rows[b] = rows

        def prepare_cloud(b):
            rows = x_rows[b]
            grouped = work.tile([P, WEIGHTINGS * FEATS * SLOTS], BF16, tag="x_grouped", align_bytes=64)
            nc.vector.tensor_copy(
                out=grouped[:].rearrange("c (w d t) -> c w d t", w=WEIGHTINGS, t=SLOTS),
                in_=rows[:].rearrange("c (w t d) -> c w d t", w=WEIGHTINGS, t=SLOTS),
            )
            codes = work.tile([P, WEIGHTINGS * FEATS], U32, tag="x_codes", align_bytes=64)
            scales = work.tile([P, WEIGHTINGS * FEATS], U8, tag="x_scales", align_bytes=64)
            nc.vector.quantize_mx(out=codes[:].bitcast(FP8X4), scales=scales[:], in_=grouped[:])
            x_mx[b] = (codes, scales)

            bank = mx_psum.tile([P, BANK], F32, tag="mx")
            for w in range(WEIGHTINGS):
                for t in range(SLOTS):
                    first = (w * SLOTS + t) * FEATS
                    nc.tensor.matmul(
                        out=bank[:, w * ONES_COLS : (w + 1) * ONES_COLS],
                        lhsT=rows[:, first : first + FEATS],
                        rhs=ones[:],
                        start=(t == 0),
                        stop=(t == SLOTS - 1),
                    )
            nc.scalar.copy(
                out=sums_by_set[:, b * WEIGHTINGS : (b + 1) * WEIGHTINGS, 0],
                in_=bank[:, 0 : WEIGHTINGS * ONES_COLS].rearrange("d (w r) -> d w r", r=ONES_COLS)[:, :, 0],
            )

        def load_set(s):
            b, w = divmod(s, WEIGHTINGS)
            power_rows[s] = {}
            for j in OPERATOR_ORDER:
                rows = load.tile([P, ROWS * POINTS], BF16, tag="power%d" % j)
                nc.sync.dma_start(
                    out=rows[:].rearrange("q (v r) -> q v r", v=HALVES),
                    in_=operators[j][b, w].rearrange("(v q i) m -> q v (i m)", v=HALVES, i=2),
                )
                power_rows[s][j] = rows

        def transpose_pairs(pairs):
            bank = pair_psum.tile([P, BANK], F32, tag="pairs")
            for g in range(QUARTERS):
                cols = slice(g * P, (g + 1) * P)
                nc.tensor.transpose(out=bank[:, cols], in_=pairs[:, cols], identity=identity[:])
            return bank

        def half_cols(v):
            return slice(v * 2 * BANK, (v + 1) * 2 * BANK)

        def transpose_operator(s, j):
            pairs = power_rows[s][j][:].bitcast(F32)
            return [transpose_pairs(pairs[:, v * BANK : (v + 1) * BANK]) for v in range(HALVES)]

        def move_to_sbuf(banks, tag):
            moved = work.tile([P, POINTS * SLOTS], BF16, tag=tag)
            for v in range(HALVES):
                nc.scalar.copy(
                    out=moved[:, half_cols(v)].bitcast(F32).rearrange("c (q g) -> c q g", g=QUARTERS),
                    in_=banks[v][:].rearrange("c (g q) -> c q g", g=QUARTERS),
                )
            return moved

        def in_sbuf(values, v):
            return values[:, half_cols(v)].rearrange("c (q g e) -> c q g e", g=QUARTERS, e=2)

        def in_psum(banks, v):
            return banks[v][:].bitcast(BF16).rearrange("c (g q e) -> c q g e", g=QUARTERS, e=2)

        def make_wavelets(s):
            psi0 = work.tile([P, POINTS * SLOTS], BF16, tag="psi0", align_bytes=64)
            psi1 = work.tile([P, POINTS * SLOTS], BF16, tag="psi1", align_bytes=64)
            psi2 = work.tile([P, POINTS * SLOTS], BF16, tag="psi2", align_bytes=64)
            p2_sbuf = move_to_sbuf(transpose_operator(s, 1), "p2_sbuf")
            p1_psum = transpose_operator(s, 0)
            for v in range(HALVES):
                nc.vector.tensor_sub(out=in_sbuf(psi0, v), in0=in_psum(p1_psum, v), in1=in_sbuf(p2_sbuf, v))
            p4_sbuf = move_to_sbuf(transpose_operator(s, 2), "p4_sbuf")
            nc.vector.tensor_sub(out=psi1[:], in0=p2_sbuf[:], in1=p4_sbuf[:])
            p8_psum = transpose_operator(s, 3)
            for v in range(HALVES):
                nc.vector.tensor_sub(out=in_sbuf(psi2, v), in0=in_sbuf(p4_sbuf, v), in1=in_psum(p8_psum, v))
            psi_grouped[s] = (psi0, psi1, psi2)

        def quantise_psi(s):
            psi_mx[s] = []
            for j in range(WAVELETS):
                codes = work.tile([P, POINTS], U32, tag="psi_codes%d" % j, align_bytes=64)
                scales = work.tile([P, POINTS], U8, tag="psi_scales%d" % j, align_bytes=64)
                nc.vector.quantize_mx(
                    out=codes[:].bitcast(FP8X4), scales=scales[:], in_=psi_grouped[s][j][:]
                )
                psi_mx[s].append((codes, scales))

        def pool_product(s, block, features, feature_cols, psi, absolute):
            bank = mx_psum.tile([P, BANK], F32, tag="mx")
            nc.tensor.matmul_mx(
                out=bank[:],
                lhsT=features[0][:, feature_cols].bitcast(FP8X4),
                lhsT_scale=features[1][:, feature_cols],
                rhs=psi[0][:].bitcast(FP8X4),
                rhs_scale=psi[1][:],
                start=True,
                stop=True,
            )
            nc.scalar.activation(
                out=absolute, in_=bank[:], func=ABS, accum_out=sums_by_set[:, s, block : block + 1]
            )

        def unread():
            absolute = work.tile([P, POINTS], BF16, tag="unread")
            return absolute[:]

        def first_layer(s):
            b, w = divmod(s, WEIGHTINGS)
            x_cols = slice(w * FEATS, (w + 1) * FEATS)
            rows = work.tile([P, 2 * POINTS], BF16, tag="f_rows")
            pool_product(s, 1, x_mx[b], x_cols, psi_mx[s][0], rows[:, 0:POINTS])
            pool_product(s, 2, x_mx[b], x_cols, psi_mx[s][1], rows[:, POINTS : 2 * POINTS])
            pool_product(s, 3, x_mx[b], x_cols, psi_mx[s][2], unread())
            f_rows[s] = rows

        def quantise_f(s):
            bank = transpose_pairs(f_rows[s][:].bitcast(F32))
            grouped = work.tile([P, 2 * FEATS * SLOTS], BF16, tag="f_grouped", align_bytes=64)
            nc.scalar.copy(
                out=grouped[:].bitcast(F32).rearrange("c (j d u) -> c j d u", j=2, u=HALVES),
                in_=bank[:].rearrange("c (j u d) -> c j d u", j=2, u=HALVES),
            )
            codes = work.tile([P, 2 * FEATS], U32, tag="f_codes", align_bytes=64)
            scales = work.tile([P, 2 * FEATS], U8, tag="f_scales", align_bytes=64)
            nc.vector.quantize_mx(out=codes[:].bitcast(FP8X4), scales=scales[:], in_=grouped[:])
            f_mx[s] = (codes, scales)

        def second_layer(s):
            block = 1 + WAVELETS
            for j in range(WAVELETS):
                for k in range(j + 1, WAVELETS):
                    pool_product(s, block, f_mx[s], slice(j * FEATS, (j + 1) * FEATS), psi_mx[s][k], unread())
                    block += 1

        def load_ahead(s):
            if s < SETS:
                if s % WEIGHTINGS == 0:
                    load_cloud(s // WEIGHTINGS)
                load_set(s)

        for s in range(LOADS_AHEAD):
            load_ahead(s)
        prepare_cloud(0)
        make_wavelets(0)
        quantise_psi(0)
        for s in range(SETS):
            following = s + 1
            load_ahead(s + LOADS_AHEAD)
            if following < SETS:
                make_wavelets(following)
            first_layer(s)
            quantise_f(s)
            if following < SETS:
                quantise_psi(following)
            if s % WEIGHTINGS == WEIGHTINGS - 2 and s + 2 < SETS:
                prepare_cloud((s + 2) // WEIGHTINGS)
            second_layer(s)

        bank = mx_psum.tile([P, BANK], F32, tag="mx")
        nc.tensor.transpose(out=bank[:, 0:P], in_=sums[:], identity=identity[:])
        means = const.tile([P, FEATS], F32)
        nc.scalar.activation(out=means[:], in_=bank[:, 0:P], func=COPY, scale=1.0 / POINTS)
        nc.sync.dma_start(
            out=out.rearrange("b (r d) -> (b r) d", d=FEATS), in_=means[0 : SETS * BLOCKS, :]
        )
